import numpy as np
import ml_dtypes


def mxq(x, axis, fmt="e4m3"):
    dtype, down = {"e4m3": (ml_dtypes.float8_e4m3fn, 7), "e5m2": (ml_dtypes.float8_e5m2, 14)}[fmt]
    v = np.moveaxis(np.asarray(x, np.float32).astype(ml_dtypes.bfloat16).astype(np.float64), axis, -1)
    blocks = v.reshape(v.shape[:-1] + (-1, 32))
    amax = np.abs(blocks).max(-1, keepdims=True)
    byte = np.maximum(np.where(amax > 0, np.frexp(amax)[1] - 1 + 127, 0) - down, 1)
    scale = np.exp2(byte - 127.0)
    codes = (blocks / scale).astype(np.float32).astype(dtype).astype(np.float64)
    return np.moveaxis((codes * scale).reshape(v.shape), -1, axis)


WIDE = False


def mx_kscale(k):
    if not WIDE:
        return np.ones(k)
    levels = np.array([20, -20, 10, -10, 0])
    a = np.random.permutation(np.resize(levels, k // 512 * 4)).reshape(k // 512, 4)
    idx = np.arange(k)
    return np.exp2(a[idx // 512, idx % 128 // 32])


BF16 = ml_dtypes.bfloat16


def bf(x):
    return np.asarray(x, np.float32).astype(BF16)


def f64(x):
    return np.asarray(x).astype(np.float64)


H, U, I, E, R = 4, 512, 4096, 512, 8

EPS = 1e-6


def cosines(X, Z):
    aff = Z @ X.T
    X_norm = np.sqrt(np.sum(X * X, axis=-1))
    Z_norm = np.sqrt(np.sum(Z * Z, axis=-1))
    return aff / (X_norm + EPS) / (Z_norm + EPS)[:, :, None]


def setup_inputs():
    s = mx_kscale(I)
    P = np.random.standard_normal((R, E)) / np.sqrt(R)
    X0 = bf(0.8 * (np.random.standard_normal((I, R)) @ P) + 0.6 * np.random.standard_normal((I, E)))
    Z = bf(0.8 * (np.random.standard_normal((H, U, R)) @ P) + 0.6 * np.random.standard_normal((H, U, E)))
    beta = bf(1.5 + 0.5 * np.random.random_sample(1))
    g = np.random.standard_normal((U, I)) * np.exp2(np.random.randint(-12, 1, (1, I))) * 256.0
    c = cosines(f64(X0), f64(Z))
    top = np.sort(c, axis=0)
    m = top[-1]
    hidx = np.argmax(c, axis=0)
    rx = 1.0 / (np.sqrt(np.sum(f64(X0) * f64(X0), axis=-1)) + EPS)
    g = np.where(top[-1] - top[-2] < 1e-5, 0.0, g)
    return {"X": bf(f64(X0) * s[:, None]), "Z": Z, "beta": beta,
            "m": np.asarray(m, np.float32), "hidx": np.asarray(hidx, np.float32), "rx": np.asarray(rx, np.float32),
            "grad_out": bf(g / s[None, :])}


def reference(X, Z, beta, m, hidx, rx, grad_out):
    X, Z, beta = f64(X), f64(Z), f64(beta)
    a = (f64(m) + 1.0) / 2.0
    dm = f64(grad_out) * (0.5 * beta * np.power(a, beta - 1.0)) * f64(rx)[None, :]
    heads = np.arange(H).reshape(H, 1, 1)
    d = np.where(f64(hidx)[None, :, :] == heads, dm[None, :, :], 0.0)
    G = mxq(d, 2, "e5m2") @ mxq(X, 0, "e4m3")
    zn = np.sqrt(np.sum(Z * Z, axis=-1, keepdims=True))
    rz = 1.0 / (zn + EPS)
    p = np.sum(G * Z, axis=-1, keepdims=True)
    return rz * (G - Z * (p * rz / zn))

@@ -1,0 +1,361 @@
+from contextlib import ExitStack
+
+import concourse.mybir as mybir
+from concourse.masks import make_identity
+
+F32 = mybir.dt.float32
+BF16 = mybir.dt.bfloat16
+U32 = mybir.dt.uint32
+U8 = mybir.dt.uint8
+E5M2_X4 = mybir.dt.float8_e5m2_x4
+E4M3_X4 = mybir.dt.float8_e4m3fn_x4
+ALU = mybir.AluOpType
+ACT = mybir.ActivationFunctionType
+
+H, U, I, E = 4, 512, 4096, 512
+EPS = 1e-6
+
+P = 128
+PACK = 4
+K_PASS = P * PACK
+PASSES = I // K_PASS
+PLANES = PASSES * PACK
+USER_BLOCKS = U // P
+UNIT_PASSES = 4
+UNIT_ITEMS = UNIT_PASSES * K_PASS
+BLOCK_UNITS = PASSES // UNIT_PASSES
+UNITS = USER_BLOCKS * BLOCK_UNITS
+BANK_PASSES = 2
+HEADS_PER_QUANTISE = 2
+
+FLOPS = 2 * H * U * I * E
+
+
+def tile_affnetr_v_kernel(tc, X, Z, beta, m, hidx, rx, grad_out, out):
+    nc = tc.nc
+    with ExitStack() as ctx:
+        consts = ctx.enter_context(tc.tile_pool(name="consts", bufs=1))
+        natural = ctx.enter_context(tc.tile_pool(name="natural", bufs=2))
+        powers = ctx.enter_context(tc.tile_pool(name="powers", bufs=2 * BLOCK_UNITS))
+        heads = ctx.enter_context(tc.tile_pool(name="heads", bufs=2 * BLOCK_UNITS))
+        work = ctx.enter_context(tc.tile_pool(name="work", bufs=2))
+        x_stage = ctx.enter_context(tc.tile_pool(name="x_stage", bufs=2))
+        x_keep = ctx.enter_context(tc.tile_pool(name="x_keep", bufs=1))
+        z_keep = ctx.enter_context(tc.tile_pool(name="z_keep", bufs=USER_BLOCKS))
+        results = ctx.enter_context(tc.tile_pool(name="results", bufs=USER_BLOCKS))
+        sums = ctx.enter_context(tc.psum_pool(name="sums", bufs=1))
+        turned = ctx.enter_context(tc.psum_pool(name="turned", bufs=2))
+        ctx.enter_context(tc.manual_schedule())
+
+        def unit_rows(k):
+            block = k // BLOCK_UNITS
+            return slice(block * P, (block + 1) * P)
+
+        def unit_cols(k):
+            part = k % BLOCK_UNITS
+            return slice(part * UNIT_ITEMS, (part + 1) * UNIT_ITEMS)
+
+        ident_f = consts.tile([P, P], F32, name="ident_f")
+        make_identity(nc, ident_f[:])
+        ident_b = consts.tile([P, P], BF16, name="ident_b")
+        make_identity(nc, ident_b[:])
+        exponents = consts.tile([P, 3, H], F32, name="exponents")
+        nc.gpsimd.memset(exponents[:, 0, :], 0.5)
+        nc.gpsimd.memset(exponents[:, 1, :], -1.0)
+        nc.gpsimd.memset(exponents[:, 2, :], -0.5)
+
+        half = consts.tile([P, 1], F32, name="half")
+        nc.vector.memset(half[:], 0.5)
+        rx_rows = consts.tile([P, P], F32, name="rx_rows")
+        nc.vector.memset(rx_rows[:], 0.0)
+        nc.scalar.dma_start(out=rx_rows[0:PLANES, :], in_=rx.rearrange("(j p) -> j p", p=P))
+        beta_b = consts.tile([P, 1], BF16, name="beta_b")
+        nc.scalar.dma_start(out=beta_b[:], in_=beta.partition_broadcast(P))
+        beta_f = consts.tile([P, 1], F32, name="beta_f")
+        nc.vector.tensor_copy(out=beta_f[:], in_=beta_b[:])
+        beta_m1 = consts.tile([P, 1], F32, name="beta_m1")
+        nc.vector.tensor_scalar_add(out=beta_m1[:], in0=beta_f[:], scalar1=-1.0)
+        factor = consts.tile([P, PLANES], F32, name="factor")
+        ln_factor = consts.tile([P, PLANES], F32, name="ln_factor")
+
+        x_view = X.rearrange("(g t p) e -> p g t e", t=PACK, p=P)
+        x_codes = x_keep.tile([P, PASSES, E], U32, name="x_codes", align_bytes=64)
+        x_scales = x_keep.tile([P, PASSES, E], U8, name="x_scales", align_bytes=64)
+
+        x_raw, x_grouped = {}, {}
+        m_nat, h_nat, g_nat, z_rows = {}, {}, {}, {}
+        power, head_of, g_banks = {}, {}, {}
+        d_all, per_head, d_codes, d_scales = {}, {}, {}, {}
+        g_sums, q_scale, neg_rz, q_dot, rest = {}, {}, {}, {}, {}
+
+        def load_x(g):
+            x_raw[g] = x_stage.tile([P, PACK, E], BF16, name="x_raw", tag="x_raw", bufs=UNIT_PASSES)
+            nc.sync.dma_start(out=x_raw[g][:], in_=x_view[:, g])
+
+        def load_m(k):
+            m_nat[k] = natural.tile([P, UNIT_ITEMS], F32, name="m_nat", tag="m_nat")
+            nc.sync.dma_start(out=m_nat[k][:], in_=m[unit_rows(k), unit_cols(k)])
+
+        def load_hidx(k):
+            h_nat[k] = natural.tile([P, UNIT_ITEMS], F32, name="h_nat", tag="h_nat")
+            nc.sync.dma_start(out=h_nat[k][:], in_=hidx[unit_rows(k), unit_cols(k)])
+
+        def load_grad(k):
+            g_nat[k] = natural.tile([P, UNIT_ITEMS], BF16, name="g_nat", tag="g_nat")
+            nc.sync.dma_start(out=g_nat[k][:], in_=grad_out[unit_rows(k), unit_cols(k)])
+
+        def load_z(block):
+            z_rows[block] = z_keep.tile([P, H, E], BF16, name="z_rows", tag="z_rows")
+            rows = slice(block * P, (block + 1) * P)
+            nc.sync.dma_start(out=z_rows[block][:], in_=Z[:, rows, :].rearrange("h p e -> p h e"))
+
+        def group_x(g):
+            x_grouped[g] = x_stage.tile([P, E, PACK], BF16, name="x_grouped", tag="x_grouped", align_bytes=64)
+            nc.vector.tensor_copy(
+                out=x_grouped[g][:].rearrange("p (c i) t -> p c t i", i=4),
+                in_=x_raw[g][:].rearrange("p t (c i) -> p c t i", i=4),
+            )
+
+        def quantise_x(g):
+            nc.vector.quantize_mx(
+                out=x_codes[:, g, :].bitcast(E4M3_X4),
+                scales=x_scales[:, g, :],
+                in_=x_grouped[g][:].rearrange("p e t -> p (e t)"),
+            )
+
+        def turn_into_bank(source, g):
+            bank = turned.tile([P, PACK, P], F32, name="bank", tag="bank")
+            for t in range(PACK):
+                first = g * K_PASS + t * P
+                nc.tensor.transpose(bank[:, t, :], source[:, first : first + P], ident_f[:])
+            return bank
+
+        def logarithms(k):
+            power[k] = powers.tile([P, UNIT_PASSES, PACK, P], F32, name="power", tag="power")
+            for g in range(UNIT_PASSES):
+                bank = turn_into_bank(m_nat[k], g)
+                nc.scalar.activation(out=power[k][:, g], in_=bank[:], func=ACT.Ln, scale=0.5, bias=half[:, 0:1])
+
+        def exponentials(k):
+            first_plane = (k % BLOCK_UNITS) * UNIT_PASSES * PACK
+            for g in range(UNIT_PASSES):
+                for t in range(PACK):
+                    j = first_plane + g * PACK + t
+                    nc.scalar.activation(
+                        out=power[k][:, g, t, :],
+                        in_=power[k][:, g, t, :],
+                        func=ACT.Exp,
+                        scale=beta_m1[:, 0:1],
+                        bias=ln_factor[:, j : j + 1],
+                    )
+
+        def winning_heads(k):
+            head_of[k] = heads.tile([P, UNIT_PASSES, P, PACK], BF16, name="head_of", tag="head_of")
+            for g in range(UNIT_PASSES):
+                bank = turn_into_bank(h_nat[k], g)
+                nc.scalar.copy(out=head_of[k][:, g], in_=bank[:].rearrange("p t u -> p u t"))
+
+        def turn_grad(k):
+            g_banks[k] = []
+            for b in range(UNIT_PASSES // BANK_PASSES):
+                bank = turned.tile([P, BANK_PASSES, PACK, P], BF16, name="g_bank", tag="g_bank")
+                for g in range(BANK_PASSES):
+                    for t in range(PACK):
+                        first = (b * BANK_PASSES + g) * K_PASS + t * P
+                        nc.tensor.transpose(bank[:, g, t, :], g_nat[k][:, first : first + P], ident_b[:])
+                g_banks[k].append(bank)
+
+        def products(k):
+            d_all[k] = work.tile([P, UNIT_PASSES, P, PACK], BF16, name="d_all", tag="d_all")
+            for b in range(UNIT_PASSES // BANK_PASSES):
+                some = slice(b * BANK_PASSES, (b + 1) * BANK_PASSES)
+                nc.vector.tensor_tensor(
+                    out=d_all[k][:, some],
+                    in0=power[k][:, some].rearrange("p g t u -> p g u t"),
+                    in1=g_banks[k][b][:].rearrange("p g t u -> p g u t"),
+                    op=ALU.mult,
+                )
+
+        def masks(k):
+            per_head[k] = work.tile([P, H, UNIT_ITEMS], BF16, name="per_head", tag="per_head", align_bytes=64)
+            for h in range(H):
+                nc.vector.tensor_scalar(
+                    out=per_head[k][:, h, :],
+                    in0=head_of[k][:].rearrange("p g u t -> p (g u t)"),
+                    scalar1=float(h),
+                    scalar2=None,
+                    op0=ALU.is_equal,
+                )
+
+        def masked(k):
+            for h in range(H):
+                nc.vector.tensor_tensor(
+                    out=per_head[k][:, h, :],
+                    in0=per_head[k][:, h, :],
+                    in1=d_all[k][:].rearrange("p g u t -> p (g u t)"),
+                    op=ALU.mult,
+                )
+
+        def quantise_d(k):
+            d_codes[k] = work.tile([P, H, UNIT_PASSES, P], U32, name="d_codes", tag="d_codes", align_bytes=64)
+            d_scales[k] = work.tile([P, H, UNIT_PASSES, P], U8, name="d_scales", tag="d_scales", align_bytes=64)
+            for first in range(0, H, HEADS_PER_QUANTISE):
+                some = slice(first, first + HEADS_PER_QUANTISE)
+                nc.vector.quantize_mx(
+                    out=d_codes[k][:, some].rearrange("p h g u -> p (h g u)").bitcast(E5M2_X4),
+                    scales=d_scales[k][:, some].rearrange("p h g u -> p (h g u)"),
+                    in_=per_head[k][:, some, :].rearrange("p h n -> p (h n)"),
+                )
+
+        def multiply(k):
+            block = k // BLOCK_UNITS
+            if k % BLOCK_UNITS == 0:
+                g_sums[block] = [sums.tile([P, E], F32, name="g_sum%d" % h, tag="g_sum%d" % h) for h in range(H)]
+            for h in range(H):
+                for g in range(UNIT_PASSES):
+                    g_all = (k % BLOCK_UNITS) * UNIT_PASSES + g
+                    nc.tensor.matmul_mx(
+                        out=g_sums[block][h][:],
+                        lhsT=d_codes[k][:, h, g, :].bitcast(E5M2_X4),
+                        lhsT_scale=d_scales[k][:, h, g, :],
+                        rhs=x_codes[:, g_all, :].bitcast(E4M3_X4),
+                        rhs_scale=x_scales[:, g_all, :],
+                        start=(g_all == 0),
+                        stop=(g_all == PASSES - 1),
+                    )
+
+        def z_norms(block):
+            zn2 = results.tile([P, H], F32, name="zn2", tag="zn2")
+            for h in range(H):
+                squares = results.tile([P, E], BF16, name="squares", tag="squares", bufs=2)
+                nc.scalar.activation(
+                    out=squares[:], in_=z_rows[block][:, h, :], func=ACT.Square, accum_out=zn2[:, h : h + 1]
+                )
+            zn_eps = results.tile([P, H], F32, name="zn_eps", tag="zn_eps")
+            nc.gpsimd.tensor_tensor(out=zn_eps[:], in0=zn2[:], in1=exponents[:, 0, :], op=ALU.pow)
+            nc.gpsimd.tensor_scalar_add(out=zn_eps[:], in0=zn_eps[:], scalar1=EPS)
+            rz = results.tile([P, H], F32, name="rz", tag="rz")
+            nc.gpsimd.tensor_tensor(out=rz[:], in0=zn_eps[:], in1=exponents[:, 1, :], op=ALU.pow)
+            q_scale[block] = results.tile([P, H], F32, name="q_scale", tag="q_scale")
+            nc.gpsimd.tensor_tensor(out=q_scale[block][:], in0=zn2[:], in1=exponents[:, 2, :], op=ALU.pow)
+            nc.gpsimd.tensor_tensor(out=q_scale[block][:], in0=q_scale[block][:], in1=rz[:], op=ALU.mult)
+            neg_rz[block] = results.tile([P, H], F32, name="neg_rz", tag="neg_rz")
+            nc.gpsimd.tensor_scalar_mul(out=neg_rz[block][:], in0=rz[:], scalar1=-1.0)
+
+        def project(block):
+            q_dot[block] = results.tile([P, H], F32, name="q_dot", tag="q_dot")
+            rest[block] = []
+            for h in range(H):
+                unread = results.tile([P, E], BF16, name="unread", tag="unread", bufs=2)
+                nc.vector.scalar_tensor_tensor(
+                    out=unread[:],
+                    in0=g_sums[block][h][:],
+                    scalar=q_scale[block][:, h : h + 1],
+                    in1=z_rows[block][:, h, :],
+                    op0=ALU.mult,
+                    op1=ALU.mult,
+                    accum_out=q_dot[block][:, h : h + 1],
+                )
+            for h in range(H):
+                rest[block].append(results.tile([P, E], F32, name="rest", tag="rest"))
+                nc.vector.scalar_tensor_tensor(
+                    out=rest[block][h][:],
+                    in0=z_rows[block][:, h, :],
+                    scalar=q_dot[block][:, h : h + 1],
+                    in1=g_sums[block][h][:],
+                    op0=ALU.mult,
+                    op1=ALU.subtract,
+                )
+
+        def finish(block):
+            rows = slice(block * P, (block + 1) * P)
+            for h in range(H):
+                nc.scalar.activation(
+                    out=rest[block][h][:], in_=rest[block][h][:], func=ACT.Copy, scale=neg_rz[block][:, h : h + 1]
+                )
+                nc.scalar.dma_start(out=out[h, rows, :], in_=rest[block][h][:])
+
+        load_m(0)
+        load_m(1)
+        for g in range(UNIT_PASSES):
+            load_x(g)
+        load_grad(0)
+        load_hidx(0)
+        load_hidx(1)
+        load_grad(1)
+        for g in range(UNIT_PASSES, PASSES):
+            load_x(g)
+        load_z(0)
+
+        rx_bank = turned.tile([P, PACK, P], F32, name="bank", tag="bank")
+        nc.tensor.transpose(rx_bank[:, 0, :], rx_rows[:], ident_f[:])
+        nc.vector.tensor_scalar(
+            out=factor[:],
+            in0=rx_bank[:, 0, 0:PLANES],
+            scalar1=beta_f[:, 0:1],
+            scalar2=0.5,
+            op0=ALU.mult,
+            op1=ALU.mult,
+        )
+
+        group_x(0)
+        for g in range(1, UNIT_PASSES):
+            group_x(g)
+            quantise_x(g - 1)
+        quantise_x(UNIT_PASSES - 1)
+
+        logarithms(0)
+        logarithms(1)
+        nc.scalar.activation(out=ln_factor[:], in_=factor[:], func=ACT.Ln)
+        load_m(2)
+        load_m(3)
+        turn_grad(0)
+        exponentials(0)
+        winning_heads(0)
+        exponentials(1)
+        winning_heads(1)
+        load_hidx(2)
+        load_hidx(3)
+        z_norms(0)
+
+        for k in range(UNITS + 1):
+            block = k // BLOCK_UNITS
+            opens_block = k % BLOCK_UNITS == 0
+            if k >= 1:
+                multiply(k - 1)
+            if k + 1 < UNITS:
+                turn_grad(k + 1)
+            if k + 2 < UNITS:
+                load_grad(k + 2)
+            if k < UNITS:
+                products(k)
+                masks(k)
+                masked(k)
+            if opens_block and block >= 1:
+                project(block - 1)
+            if k < UNITS:
+                quantise_d(k)
+            if k == 0:
+                group_x(UNIT_PASSES)
+                for g in range(UNIT_PASSES + 1, PASSES):
+                    group_x(g)
+                    quantise_x(g - 1)
+                quantise_x(PASSES - 1)
+            if opens_block:
+                if block + 1 < USER_BLOCKS:
+                    load_z(block + 1)
+                    logarithms(k + 2)
+                    logarithms(k + 3)
+                    winning_heads(k + 2)
+                    winning_heads(k + 3)
+                    z_norms(block + 1)
+                if block + 2 < USER_BLOCKS:
+                    load_m(k + 4)
+                    load_m(k + 5)
+                    load_hidx(k + 4)
+                    load_hidx(k + 5)
+                if block >= 1:
+                    finish(block - 1)
+            elif block + 1 < USER_BLOCKS:
+                exponentials(k + 1)
+                exponentials(k + 2)

@@ -68,9 +68,9 @@ def tile_affnetr_v_kernel(tc, X, Z, beta, m, hidx, rx, grad_out, out):
         nc.vector.memset(half[:], 0.5)
         rx_rows = consts.tile([P, P], F32, name="rx_rows")
         nc.vector.memset(rx_rows[:], 0.0)
-        nc.scalar.dma_start(out=rx_rows[0:PLANES, :], in_=rx.rearrange("(j p) -> j p", p=P))
+        nc.sync.dma_start(out=rx_rows[0:PLANES, :], in_=rx.rearrange("(j p) -> j p", p=P))
         beta_b = consts.tile([P, 1], BF16, name="beta_b")
-        nc.scalar.dma_start(out=beta_b[:], in_=beta.partition_broadcast(P))
+        nc.sync.dma_start(out=beta_b[:], in_=beta.partition_broadcast(P))
         beta_f = consts.tile([P, 1], F32, name="beta_f")
         nc.vector.tensor_copy(out=beta_f[:], in_=beta_b[:])
         beta_m1 = consts.tile([P, 1], F32, name="beta_m1")
@@ -188,13 +188,12 @@ def tile_affnetr_v_kernel(tc, X, Z, beta, m, hidx, rx, grad_out, out):
                 )
 
         def masked(k):
-            for h in range(H):
-                nc.vector.tensor_tensor(
-                    out=per_head[k][:, h, :],
-                    in0=per_head[k][:, h, :],
-                    in1=d_all[k][:].rearrange("p g u t -> p (g u t)"),
-                    op=ALU.mult,
-                )
+            nc.vector.tensor_tensor(
+                out=per_head[k][:],
+                in0=per_head[k][:],
+                in1=d_all[k][:].rearrange("p g u t -> p (g u t)").unsqueeze(1).to_broadcast([P, H, UNIT_ITEMS]),
+                op=ALU.mult,
+            )
 
         def quantise_d(k):
             d_codes[k] = work.tile([P, H, UNIT_PASSES, P], U32, name="d_codes", tag="d_codes", align_bytes=64)
@@ -245,27 +244,28 @@ def tile_affnetr_v_kernel(tc, X, Z, beta, m, hidx, rx, grad_out, out):
         def project(block):
             q_dot[block] = results.tile([P, H], F32, name="q_dot", tag="q_dot")
             rest[block] = []
-            for h in range(H):
-                unread = results.tile([P, E], BF16, name="unread", tag="unread", bufs=2)
-                nc.vector.scalar_tensor_tensor(
-                    out=unread[:],
-                    in0=g_sums[block][h][:],
-                    scalar=q_scale[block][:, h : h + 1],
-                    in1=z_rows[block][:, h, :],
-                    op0=ALU.mult,
-                    op1=ALU.mult,
-                    accum_out=q_dot[block][:, h : h + 1],
-                )
-            for h in range(H):
-                rest[block].append(results.tile([P, E], F32, name="rest", tag="rest"))
-                nc.vector.scalar_tensor_tensor(
-                    out=rest[block][h][:],
-                    in0=z_rows[block][:, h, :],
-                    scalar=q_dot[block][:, h : h + 1],
-                    in1=g_sums[block][h][:],
-                    op0=ALU.mult,
-                    op1=ALU.subtract,
-                )
+            for first in range(0, H, 2):
+                for h in range(first, first + 2):
+                    unread = results.tile([P, E], BF16, name="unread", tag="unread", bufs=2)
+                    nc.vector.scalar_tensor_tensor(
+                        out=unread[:],
+                        in0=g_sums[block][h][:],
+                        scalar=q_scale[block][:, h : h + 1],
+                        in1=z_rows[block][:, h, :],
+                        op0=ALU.mult,
+                        op1=ALU.mult,
+                        accum_out=q_dot[block][:, h : h + 1],
+                    )
+                for h in range(first, first + 2):
+                    rest[block].append(results.tile([P, E], F32, name="rest", tag="rest"))
+                    nc.vector.scalar_tensor_tensor(
+                        out=rest[block][h][:],
+                        in0=z_rows[block][:, h, :],
+                        scalar=q_dot[block][:, h : h + 1],
+                        in1=g_sums[block][h][:],
+                        op0=ALU.mult,
+                        op1=ALU.subtract,
+                    )
 
         def finish(block):
             rows = slice(block * P, (block + 1) * P)
@@ -287,6 +287,7 @@ def tile_affnetr_v_kernel(tc, X, Z, beta, m, hidx, rx, grad_out, out):
             load_x(g)
         load_z(0)
 
+        logarithms(0)
         rx_bank = turned.tile([P, PACK, P], F32, name="bank", tag="bank")
         nc.tensor.transpose(rx_bank[:, 0, :], rx_rows[:], ident_f[:])
         nc.vector.tensor_scalar(
@@ -297,6 +298,8 @@ def tile_affnetr_v_kernel(tc, X, Z, beta, m, hidx, rx, grad_out, out):
             op0=ALU.mult,
             op1=ALU.mult,
         )
+        logarithms(1)
+        nc.scalar.activation(out=ln_factor[:], in_=factor[:], func=ACT.Ln)
 
         group_x(0)
         for g in range(1, UNIT_PASSES):
@@ -304,9 +307,6 @@ def tile_affnetr_v_kernel(tc, X, Z, beta, m, hidx, rx, grad_out, out):
             quantise_x(g - 1)
         quantise_x(UNIT_PASSES - 1)
 
-        logarithms(0)
-        logarithms(1)
-        nc.scalar.activation(out=ln_factor[:], in_=factor[:], func=ACT.Ln)
         load_m(2)
         load_m(3)
         turn_grad(0)
@@ -316,7 +316,6 @@ def tile_affnetr_v_kernel(tc, X, Z, beta, m, hidx, rx, grad_out, out):
         winning_heads(1)
         load_hidx(2)
         load_hidx(3)
-        z_norms(0)
 
         for k in range(UNITS + 1):
             block = k // BLOCK_UNITS
@@ -348,7 +347,10 @@ def tile_affnetr_v_kernel(tc, X, Z, beta, m, hidx, rx, grad_out, out):
                     logarithms(k + 3)
                     winning_heads(k + 2)
                     winning_heads(k + 3)
-                    z_norms(block + 1)
+                    exponentials(k + 2)
+                    exponentials(k + 3)
+                if block < USER_BLOCKS:
+                    z_norms(block)
                 if block + 2 < USER_BLOCKS:
                     load_m(k + 4)
                     load_m(k + 5)
@@ -356,6 +358,3 @@ def tile_affnetr_v_kernel(tc, X, Z, beta, m, hidx, rx, grad_out, out):
                     load_hidx(k + 5)
                 if block >= 1:
                     finish(block - 1)
-            elif block + 1 < USER_BLOCKS:
-                exponentials(k + 1)
-                exponentials(k + 2)

@@ -131,10 +131,12 @@ def tile_affnetr_v_kernel(tc, X, Z, beta, m, hidx, rx, grad_out, out):
             return bank
 
         def logarithms(k):
-            power[k] = powers.tile([P, UNIT_PASSES, PACK, P], F32, name="power", tag="power")
+            power[k] = powers.tile([P, PACK, UNIT_PASSES, P], F32, name="power", tag="power")
             for g in range(UNIT_PASSES):
                 bank = turn_into_bank(m_nat[k], g)
-                nc.scalar.activation(out=power[k][:, g], in_=bank[:], func=ACT.Ln, scale=0.5, bias=half[:, 0:1])
+                nc.scalar.activation(
+                    out=power[k][:, :, g, :], in_=bank[:], func=ACT.Ln, scale=0.5, bias=half[:, 0:1]
+                )
 
         def exponentials(k):
             first_plane = (k % BLOCK_UNITS) * UNIT_PASSES * PACK
@@ -142,8 +144,8 @@ def tile_affnetr_v_kernel(tc, X, Z, beta, m, hidx, rx, grad_out, out):
                 for t in range(PACK):
                     j = first_plane + g * PACK + t
                     nc.scalar.activation(
-                        out=power[k][:, g, t, :],
-                        in_=power[k][:, g, t, :],
+                        out=power[k][:, t, g, :],
+                        in_=power[k][:, t, g, :],
                         func=ACT.Exp,
                         scale=beta_m1[:, 0:1],
                         bias=ln_factor[:, j : j + 1],
@@ -158,11 +160,11 @@ def tile_affnetr_v_kernel(tc, X, Z, beta, m, hidx, rx, grad_out, out):
         def turn_grad(k):
             g_banks[k] = []
             for b in range(UNIT_PASSES // BANK_PASSES):
-                bank = turned.tile([P, BANK_PASSES, PACK, P], BF16, name="g_bank", tag="g_bank")
+                bank = turned.tile([P, PACK, BANK_PASSES, P], BF16, name="g_bank", tag="g_bank")
                 for g in range(BANK_PASSES):
                     for t in range(PACK):
                         first = (b * BANK_PASSES + g) * K_PASS + t * P
-                        nc.tensor.transpose(bank[:, g, t, :], g_nat[k][:, first : first + P], ident_b[:])
+                        nc.tensor.transpose(bank[:, t, g, :], g_nat[k][:, first : first + P], ident_b[:])
                 g_banks[k].append(bank)
 
         def products(k):
@@ -170,9 +172,9 @@ def tile_affnetr_v_kernel(tc, X, Z, beta, m, hidx, rx, grad_out, out):
             for b in range(UNIT_PASSES // BANK_PASSES):
                 some = slice(b * BANK_PASSES, (b + 1) * BANK_PASSES)
                 nc.vector.tensor_tensor(
-                    out=d_all[k][:, some],
-                    in0=power[k][:, some].rearrange("p g t u -> p g u t"),
-                    in1=g_banks[k][b][:].rearrange("p g t u -> p g u t"),
+                    out=d_all[k][:, some].rearrange("p g (c i) t -> p (g c) t i", i=4),
+                    in0=power[k][:, :, some, :].rearrange("p t g (c i) -> p (g c) t i", i=4),
+                    in1=g_banks[k][b][:].rearrange("p t g (c i) -> p (g c) t i", i=4),
                     op=ALU.mult,
                 )
 
@@ -188,12 +190,13 @@ def tile_affnetr_v_kernel(tc, X, Z, beta, m, hidx, rx, grad_out, out):
                 )
 
         def masked(k):
-            nc.vector.tensor_tensor(
-                out=per_head[k][:],
-                in0=per_head[k][:],
-                in1=d_all[k][:].rearrange("p g u t -> p (g u t)").unsqueeze(1).to_broadcast([P, H, UNIT_ITEMS]),
-                op=ALU.mult,
-            )
+            for h in range(H):
+                nc.vector.tensor_tensor(
+                    out=per_head[k][:, h, :],
+                    in0=per_head[k][:, h, :],
+                    in1=d_all[k][:].rearrange("p g u t -> p (g u t)"),
+                    op=ALU.mult,
+                )
 
         def quantise_d(k):
             d_codes[k] = work.tile([P, H, UNIT_PASSES, P], U32, name="d_codes", tag="d_codes", align_bytes=64)
@@ -316,6 +319,7 @@ def tile_affnetr_v_kernel(tc, X, Z, beta, m, hidx, rx, grad_out, out):
         winning_heads(1)
         load_hidx(2)
         load_hidx(3)
+        z_norms(0)
 
         for k in range(UNITS + 1):
             block = k // BLOCK_UNITS
@@ -349,8 +353,7 @@ def tile_affnetr_v_kernel(tc, X, Z, beta, m, hidx, rx, grad_out, out):
                     winning_heads(k + 3)
                     exponentials(k + 2)
                     exponentials(k + 3)
-                if block < USER_BLOCKS:
-                    z_norms(block)
+                    z_norms(block + 1)
                 if block + 2 < USER_BLOCKS:
                     load_m(k + 4)
                     load_m(k + 5)

@@ -28,6 +28,8 @@ UNITS = USER_BLOCKS * BLOCK_UNITS
 BANK_PASSES = 2
 HEADS_PER_QUANTISE = 2
 
+SCALAR_MASKS = {UNITS - 2: (0, H - 1), UNITS - 1: (0, H - 1, 1, 2)}
+
 FLOPS = 2 * H * U * I * E
 
 
@@ -44,7 +46,7 @@ def tile_affnetr_v_kernel(tc, X, Z, beta, m, hidx, rx, grad_out, out):
         z_keep = ctx.enter_context(tc.tile_pool(name="z_keep", bufs=USER_BLOCKS))
         results = ctx.enter_context(tc.tile_pool(name="results", bufs=USER_BLOCKS))
         sums = ctx.enter_context(tc.psum_pool(name="sums", bufs=1))
-        turned = ctx.enter_context(tc.psum_pool(name="turned", bufs=2))
+        turned = ctx.enter_context(tc.psum_pool(name="turned", bufs=4))
         ctx.enter_context(tc.manual_schedule())
 
         def unit_rows(k):
@@ -66,6 +68,11 @@ def tile_affnetr_v_kernel(tc, X, Z, beta, m, hidx, rx, grad_out, out):
 
         half = consts.tile([P, 1], F32, name="half")
         nc.vector.memset(half[:], 0.5)
+        plus_one = consts.tile([P, 1], F32, name="plus_one")
+        nc.vector.memset(plus_one[:], 1.0)
+        minus_h = consts.tile([P, H], F32, name="minus_h")
+        for h in range(H):
+            nc.vector.memset(minus_h[:, h : h + 1], float(-h))
         rx_rows = consts.tile([P, P], F32, name="rx_rows")
         nc.vector.memset(rx_rows[:], 0.0)
         nc.sync.dma_start(out=rx_rows[0:PLANES, :], in_=rx.rearrange("(j p) -> j p", p=P))
@@ -124,7 +131,7 @@ def tile_affnetr_v_kernel(tc, X, Z, beta, m, hidx, rx, grad_out, out):
             )
 
         def turn_into_bank(source, g):
-            bank = turned.tile([P, PACK, P], F32, name="bank", tag="bank")
+            bank = turned.tile([P, PACK, P], F32, name="bank", tag="turned")
             for t in range(PACK):
                 first = g * K_PASS + t * P
                 nc.tensor.transpose(bank[:, t, :], source[:, first : first + P], ident_f[:])
@@ -160,7 +167,10 @@ def tile_affnetr_v_kernel(tc, X, Z, beta, m, hidx, rx, grad_out, out):
         def turn_grad(k):
             g_banks[k] = []
             for b in range(UNIT_PASSES // BANK_PASSES):
-                bank = turned.tile([P, PACK, BANK_PASSES, P], BF16, name="g_bank", tag="g_bank")
+                if k == 0:
+                    bank = sums.tile([P, PACK, BANK_PASSES, P], BF16, name="g_first%d" % b, tag="g_sum%d" % b)
+                else:
+                    bank = turned.tile([P, PACK, BANK_PASSES, P], BF16, name="g_bank", tag="turned")
                 for g in range(BANK_PASSES):
                     for t in range(PACK):
                         first = (b * BANK_PASSES + g) * K_PASS + t * P
@@ -180,14 +190,33 @@ def tile_affnetr_v_kernel(tc, X, Z, beta, m, hidx, rx, grad_out, out):
 
         def masks(k):
             per_head[k] = work.tile([P, H, UNIT_ITEMS], BF16, name="per_head", tag="per_head", align_bytes=64)
+            flat = head_of[k][:].rearrange("p g u t -> p (g u t)")
             for h in range(H):
+                if h in SCALAR_MASKS.get(k, ()):
+                    continue
                 nc.vector.tensor_scalar(
-                    out=per_head[k][:, h, :],
-                    in0=head_of[k][:].rearrange("p g u t -> p (g u t)"),
-                    scalar1=float(h),
-                    scalar2=None,
-                    op0=ALU.is_equal,
+                    out=per_head[k][:, h, :], in0=flat, scalar1=float(h), scalar2=None, op0=ALU.is_equal
                 )
+            for h in SCALAR_MASKS.get(k, ()):
+                if h == 0:
+                    nc.scalar.activation(
+                        out=per_head[k][:, h, :], in_=flat, func=ACT.Relu, scale=-1.0, bias=plus_one[:, 0:1]
+                    )
+                elif h == H - 1:
+                    nc.scalar.activation(
+                        out=per_head[k][:, h, :], in_=flat, func=ACT.Relu, scale=1.0, bias=minus_h[:, H - 2 : H - 1]
+                    )
+                else:
+                    nc.scalar.activation(
+                        out=per_head[k][:, h, :], in_=flat, func=ACT.Square, scale=1.0, bias=minus_h[:, h : h + 1]
+                    )
+                    nc.scalar.activation(
+                        out=per_head[k][:, h, :],
+                        in_=per_head[k][:, h, :],
+                        func=ACT.Relu,
+                        scale=-1.0,
+                        bias=plus_one[:, 0:1],
+                    )
 
         def masked(k):
             for h in range(H):
@@ -278,20 +307,23 @@ def tile_affnetr_v_kernel(tc, X, Z, beta, m, hidx, rx, grad_out, out):
                 )
                 nc.scalar.dma_start(out=out[h, rows, :], in_=rest[block][h][:])
 
+        load_x(0)
+        load_x(1)
         load_m(0)
+        load_x(2)
+        load_x(3)
         load_m(1)
-        for g in range(UNIT_PASSES):
-            load_x(g)
+        load_x(4)
         load_grad(0)
+        load_x(5)
+        load_x(6)
+        load_x(7)
         load_hidx(0)
         load_hidx(1)
         load_grad(1)
-        for g in range(UNIT_PASSES, PASSES):
-            load_x(g)
         load_z(0)
 
-        logarithms(0)
-        rx_bank = turned.tile([P, PACK, P], F32, name="bank", tag="bank")
+        rx_bank = turned.tile([P, PACK, P], F32, name="bank", tag="turned")
         nc.tensor.transpose(rx_bank[:, 0, :], rx_rows[:], ident_f[:])
         nc.vector.tensor_scalar(
             out=factor[:],
@@ -301,14 +333,15 @@ def tile_affnetr_v_kernel(tc, X, Z, beta, m, hidx, rx, grad_out, out):
             op0=ALU.mult,
             op1=ALU.mult,
         )
-        logarithms(1)
         nc.scalar.activation(out=ln_factor[:], in_=factor[:], func=ACT.Ln)
+        logarithms(0)
+        logarithms(1)
 
         group_x(0)
-        for g in range(1, UNIT_PASSES):
+        for g in range(1, PASSES):
             group_x(g)
             quantise_x(g - 1)
-        quantise_x(UNIT_PASSES - 1)
+        quantise_x(PASSES - 1)
 
         load_m(2)
         load_m(3)
@@ -319,45 +352,55 @@ def tile_affnetr_v_kernel(tc, X, Z, beta, m, hidx, rx, grad_out, out):
         winning_heads(1)
         load_hidx(2)
         load_hidx(3)
-        z_norms(0)
 
         for k in range(UNITS + 1):
             block = k // BLOCK_UNITS
             opens_block = k % BLOCK_UNITS == 0
-            if k >= 1:
-                multiply(k - 1)
-            if k + 1 < UNITS:
-                turn_grad(k + 1)
+            more_blocks = block + 1 < USER_BLOCKS
+            if opens_block:
+                if more_blocks:
+                    logarithms(k + 2)
+                    logarithms(k + 3)
+                if k >= 1:
+                    multiply(k - 1)
+                if k + 1 < UNITS:
+                    turn_grad(k + 1)
+            else:
+                if k == 1:
+                    multiply(k - 1)
+                if more_blocks:
+                    winning_heads(k + 1)
+                    winning_heads(k + 2)
+                if k + 1 < UNITS:
+                    turn_grad(k + 1)
+                if k > 1:
+                    multiply(k - 1)
             if k + 2 < UNITS:
                 load_grad(k + 2)
             if k < UNITS:
                 products(k)
                 masks(k)
                 masked(k)
+                quantise_d(k)
             if opens_block and block >= 1:
                 project(block - 1)
-            if k < UNITS:
-                quantise_d(k)
-            if k == 0:
-                group_x(UNIT_PASSES)
-                for g in range(UNIT_PASSES + 1, PASSES):
-                    group_x(g)
-                    quantise_x(g - 1)
-                quantise_x(PASSES - 1)
             if opens_block:
-                if block + 1 < USER_BLOCKS:
+                if more_blocks:
                     load_z(block + 1)
-                    logarithms(k + 2)
-                    logarithms(k + 3)
-                    winning_heads(k + 2)
-                    winning_heads(k + 3)
                     exponentials(k + 2)
                     exponentials(k + 3)
-                    z_norms(block + 1)
                 if block + 2 < USER_BLOCKS:
                     load_m(k + 4)
                     load_m(k + 5)
+                if k == UNITS:
+                    finish(block - 1)
+            else:
+                if k == 1:
+                    z_norms(0)
+                if more_blocks:
+                    z_norms(block + 1)
+                if block + 2 < USER_BLOCKS:
+                    load_hidx(k + 3)
                     load_hidx(k + 4)
-                    load_hidx(k + 5)
                 if block >= 1:
                     finish(block - 1)

@@ -69,19 +69,15 @@ def tile_affnetr_v_kernel(tc, X, Z, beta, m, hidx, rx, grad_out, out):
         half = consts.tile([P, 1], F32, name="half")
         nc.vector.memset(half[:], 0.5)
         plus_one = consts.tile([P, 1], F32, name="plus_one")
-        nc.vector.memset(plus_one[:], 1.0)
+        nc.gpsimd.memset(plus_one[:], 1.0)
         minus_h = consts.tile([P, H], F32, name="minus_h")
         for h in range(H):
-            nc.vector.memset(minus_h[:, h : h + 1], float(-h))
+            nc.gpsimd.memset(minus_h[:, h : h + 1], float(-h))
         rx_rows = consts.tile([P, P], F32, name="rx_rows")
         nc.vector.memset(rx_rows[:], 0.0)
-        nc.sync.dma_start(out=rx_rows[0:PLANES, :], in_=rx.rearrange("(j p) -> j p", p=P))
         beta_b = consts.tile([P, 1], BF16, name="beta_b")
-        nc.sync.dma_start(out=beta_b[:], in_=beta.partition_broadcast(P))
         beta_f = consts.tile([P, 1], F32, name="beta_f")
-        nc.vector.tensor_copy(out=beta_f[:], in_=beta_b[:])
         beta_m1 = consts.tile([P, 1], F32, name="beta_m1")
-        nc.vector.tensor_scalar_add(out=beta_m1[:], in0=beta_f[:], scalar1=-1.0)
         factor = consts.tile([P, PLANES], F32, name="factor")
         ln_factor = consts.tile([P, PLANES], F32, name="ln_factor")
 
@@ -309,6 +305,8 @@ def tile_affnetr_v_kernel(tc, X, Z, beta, m, hidx, rx, grad_out, out):
 
         load_x(0)
         load_x(1)
+        nc.sync.dma_start(out=rx_rows[0:PLANES, :], in_=rx.rearrange("(j p) -> j p", p=P))
+        nc.sync.dma_start(out=beta_b[:], in_=beta.partition_broadcast(P))
         load_m(0)
         load_x(2)
         load_x(3)
@@ -323,6 +321,11 @@ def tile_affnetr_v_kernel(tc, X, Z, beta, m, hidx, rx, grad_out, out):
         load_grad(1)
         load_z(0)
 
+        group_x(0)
+        group_x(1)
+        quantise_x(0)
+        nc.vector.tensor_copy(out=beta_f[:], in_=beta_b[:])
+        nc.vector.tensor_scalar_add(out=beta_m1[:], in0=beta_f[:], scalar1=-1.0)
         rx_bank = turned.tile([P, PACK, P], F32, name="bank", tag="turned")
         nc.tensor.transpose(rx_bank[:, 0, :], rx_rows[:], ident_f[:])
         nc.vector.tensor_scalar(
@@ -333,12 +336,10 @@ def tile_affnetr_v_kernel(tc, X, Z, beta, m, hidx, rx, grad_out, out):
             op0=ALU.mult,
             op1=ALU.mult,
         )
-        nc.scalar.activation(out=ln_factor[:], in_=factor[:], func=ACT.Ln)
         logarithms(0)
         logarithms(1)
-
-        group_x(0)
-        for g in range(1, PASSES):
+        nc.scalar.activation(out=ln_factor[:], in_=factor[:], func=ACT.Ln)
+        for g in range(2, PASSES):
             group_x(g)
             quantise_x(g - 1)
         quantise_x(PASSES - 1)

@@ -178,9 +178,9 @@ def tile_affnetr_v_kernel(tc, X, Z, beta, m, hidx, rx, grad_out, out):
             for b in range(UNIT_PASSES // BANK_PASSES):
                 some = slice(b * BANK_PASSES, (b + 1) * BANK_PASSES)
                 nc.vector.tensor_tensor(
-                    out=d_all[k][:, some].rearrange("p g (c i) t -> p (g c) t i", i=4),
-                    in0=power[k][:, :, some, :].rearrange("p t g (c i) -> p (g c) t i", i=4),
-                    in1=g_banks[k][b][:].rearrange("p t g (c i) -> p (g c) t i", i=4),
+                    out=d_all[k][:, some].rearrange("p g (c i) t -> p (g c) t i", i=8),
+                    in0=power[k][:, :, some, :].rearrange("p t g (c i) -> p (g c) t i", i=8),
+                    in1=g_banks[k][b][:].rearrange("p t g (c i) -> p (g c) t i", i=8),
                     op=ALU.mult,
                 )
 

from contextlib import ExitStack

import concourse.mybir as mybir
from concourse.masks import make_identity

F32 = mybir.dt.float32
BF16 = mybir.dt.bfloat16
U32 = mybir.dt.uint32
U8 = mybir.dt.uint8
E5M2_X4 = mybir.dt.float8_e5m2_x4
E4M3_X4 = mybir.dt.float8_e4m3fn_x4
ALU = mybir.AluOpType
ACT = mybir.ActivationFunctionType

H, U, I, E = 4, 512, 4096, 512
EPS = 1e-6

P = 128
PACK = 4
K_PASS = P * PACK
PASSES = I // K_PASS
PLANES = PASSES * PACK
USER_BLOCKS = U // P
UNIT_PASSES = 4
UNIT_ITEMS = UNIT_PASSES * K_PASS
BLOCK_UNITS = PASSES // UNIT_PASSES
UNITS = USER_BLOCKS * BLOCK_UNITS
BANK_PASSES = 2
HEADS_PER_QUANTISE = 2

SCALAR_MASKS = {UNITS - 2: (0, H - 1), UNITS - 1: (0, H - 1, 1, 2)}

FLOPS = 2 * H * U * I * E


def tile_affnetr_v_kernel(tc, X, Z, beta, m, hidx, rx, grad_out, out):
    nc = tc.nc
    with ExitStack() as ctx:
        consts = ctx.enter_context(tc.tile_pool(name="consts", bufs=1))
        natural = ctx.enter_context(tc.tile_pool(name="natural", bufs=2))
        powers = ctx.enter_context(tc.tile_pool(name="powers", bufs=2 * BLOCK_UNITS))
        heads = ctx.enter_context(tc.tile_pool(name="heads", bufs=2 * BLOCK_UNITS))
        work = ctx.enter_context(tc.tile_pool(name="work", bufs=2))
        x_stage = ctx.enter_context(tc.tile_pool(name="x_stage", bufs=2))
        x_keep = ctx.enter_context(tc.tile_pool(name="x_keep", bufs=1))
        z_keep = ctx.enter_context(tc.tile_pool(name="z_keep", bufs=USER_BLOCKS))
        results = ctx.enter_context(tc.tile_pool(name="results", bufs=USER_BLOCKS))
        sums = ctx.enter_context(tc.psum_pool(name="sums", bufs=1))
        turned = ctx.enter_context(tc.psum_pool(name="turned", bufs=4))
        ctx.enter_context(tc.manual_schedule())

        def unit_rows(k):
            block = k // BLOCK_UNITS
            return slice(block * P, (block + 1) * P)

        def unit_cols(k):
            part = k % BLOCK_UNITS
            return slice(part * UNIT_ITEMS, (part + 1) * UNIT_ITEMS)

        ident_f = consts.tile([P, P], F32, name="ident_f")
        make_identity(nc, ident_f[:])
        ident_b = consts.tile([P, P], BF16, name="ident_b")
        make_identity(nc, ident_b[:])
        exponents = consts.tile([P, 3, H], F32, name="exponents")
        nc.gpsimd.memset(exponents[:, 0, :], 0.5)
        nc.gpsimd.memset(exponents[:, 1, :], -1.0)
        nc.gpsimd.memset(exponents[:, 2, :], -0.5)

        half = consts.tile([P, 1], F32, name="half")
        nc.vector.memset(half[:], 0.5)
        plus_one = consts.tile([P, 1], F32, name="plus_one")
        nc.gpsimd.memset(plus_one[:], 1.0)
        minus_h = consts.tile([P, H], F32, name="minus_h")
        for h in range(H):
            nc.gpsimd.memset(minus_h[:, h : h + 1], float(-h))
        rx_rows = consts.tile([P, P], F32, name="rx_rows")
        nc.vector.memset(rx_rows[:], 0.0)
        beta_b = consts.tile([P, 1], BF16, name="beta_b")
        beta_f = consts.tile([P, 1], F32, name="beta_f")
        beta_m1 = consts.tile([P, 1], F32, name="beta_m1")
        factor = consts.tile([P, PLANES], F32, name="factor")
        ln_factor = consts.tile([P, PLANES], F32, name="ln_factor")

        x_view = X.rearrange("(g t p) e -> p g t e", t=PACK, p=P)
        x_codes = x_keep.tile([P, PASSES, E], U32, name="x_codes", align_bytes=64)
        x_scales = x_keep.tile([P, PASSES, E], U8, name="x_scales", align_bytes=64)

        x_raw, x_grouped = {}, {}
        m_nat, h_nat, g_nat, z_rows = {}, {}, {}, {}
        power, head_of, g_banks = {}, {}, {}
        d_all, per_head, d_codes, d_scales = {}, {}, {}, {}
        g_sums, q_scale, neg_rz, q_dot, rest = {}, {}, {}, {}, {}

        def load_x(g):
            x_raw[g] = x_stage.tile([P, PACK, E], BF16, name="x_raw", tag="x_raw", bufs=UNIT_PASSES)
            nc.sync.dma_start(out=x_raw[g][:], in_=x_view[:, g])

        def load_m(k):
            m_nat[k] = natural.tile([P, UNIT_ITEMS], F32, name="m_nat", tag="m_nat")
            nc.sync.dma_start(out=m_nat[k][:], in_=m[unit_rows(k), unit_cols(k)])

        def load_hidx(k):
            h_nat[k] = natural.tile([P, UNIT_ITEMS], F32, name="h_nat", tag="h_nat")
            nc.sync.dma_start(out=h_nat[k][:], in_=hidx[unit_rows(k), unit_cols(k)])

        def load_grad(k):
            g_nat[k] = natural.tile([P, UNIT_ITEMS], BF16, name="g_nat", tag="g_nat")
            nc.sync.dma_start(out=g_nat[k][:], in_=grad_out[unit_rows(k), unit_cols(k)])

        def load_z(block):
            z_rows[block] = z_keep.tile([P, H, E], BF16, name="z_rows", tag="z_rows")
            rows = slice(block * P, (block + 1) * P)
            nc.sync.dma_start(out=z_rows[block][:], in_=Z[:, rows, :].rearrange("h p e -> p h e"))

        def group_x(g):
            x_grouped[g] = x_stage.tile([P, E, PACK], BF16, name="x_grouped", tag="x_grouped", align_bytes=64)
            nc.vector.tensor_copy(
                out=x_grouped[g][:].rearrange("p (c i) t -> p c t i", i=4),
                in_=x_raw[g][:].rearrange("p t (c i) -> p c t i", i=4),
            )

        def quantise_x(g):
            nc.vector.quantize_mx(
                out=x_codes[:, g, :].bitcast(E4M3_X4),
                scales=x_scales[:, g, :],
                in_=x_grouped[g][:].rearrange("p e t -> p (e t)"),
            )

        def turn_into_bank(source, g):
            bank = turned.tile([P, PACK, P], F32, name="bank", tag="turned")
            for t in range(PACK):
                first = g * K_PASS + t * P
                nc.tensor.transpose(bank[:, t, :], source[:, first : first + P], ident_f[:])
            return bank

        def logarithms(k):
            power[k] = powers.tile([P, PACK, UNIT_PASSES, P], F32, name="power", tag="power")
            for g in range(UNIT_PASSES):
                bank = turn_into_bank(m_nat[k], g)
                nc.scalar.activation(
                    out=power[k][:, :, g, :], in_=bank[:], func=ACT.Ln, scale=0.5, bias=half[:, 0:1]
                )

        def exponentials(k):
            first_plane = (k % BLOCK_UNITS) * UNIT_PASSES * PACK
            for g in range(UNIT_PASSES):
                for t in range(PACK):
                    j = first_plane + g * PACK + t
                    nc.scalar.activation(
                        out=power[k][:, t, g, :],
                        in_=power[k][:, t, g, :],
                        func=ACT.Exp,
                        scale=beta_m1[:, 0:1],
                        bias=ln_factor[:, j : j + 1],
                    )

        def winning_heads(k):
            head_of[k] = heads.tile([P, UNIT_PASSES, P, PACK], BF16, name="head_of", tag="head_of")
            for g in range(UNIT_PASSES):
                bank = turn_into_bank(h_nat[k], g)
                nc.scalar.copy(out=head_of[k][:, g], in_=bank[:].rearrange("p t u -> p u t"))

        def turn_grad(k):
            g_banks[k] = []
            for b in range(UNIT_PASSES // BANK_PASSES):
                if k == 0:
                    bank = sums.tile([P, PACK, BANK_PASSES, P], BF16, name="g_first%d" % b, tag="g_sum%d" % b)
                else:
                    bank = turned.tile([P, PACK, BANK_PASSES, P], BF16, name="g_bank", tag="turned")
                for g in range(BANK_PASSES):
                    for t in range(PACK):
                        first = (b * BANK_PASSES + g) * K_PASS + t * P
                        nc.tensor.transpose(bank[:, t, g, :], g_nat[k][:, first : first + P], ident_b[:])
                g_banks[k].append(bank)

        def products(k):
            d_all[k] = work.tile([P, UNIT_PASSES, P, PACK], BF16, name="d_all", tag="d_all")
            for b in range(UNIT_PASSES // BANK_PASSES):
                some = slice(b * BANK_PASSES, (b + 1) * BANK_PASSES)
                nc.vector.tensor_tensor(
                    out=d_all[k][:, some].rearrange("p g (c i) t -> p (g c) t i", i=8),
                    in0=power[k][:, :, some, :].rearrange("p t g (c i) -> p (g c) t i", i=8),
                    in1=g_banks[k][b][:].rearrange("p t g (c i) -> p (g c) t i", i=8),
                    op=ALU.mult,
                )

        def masks(k):
            per_head[k] = work.tile([P, H, UNIT_ITEMS], BF16, name="per_head", tag="per_head", align_bytes=64)
            flat = head_of[k][:].rearrange("p g u t -> p (g u t)")
            for h in range(H):
                if h in SCALAR_MASKS.get(k, ()):
                    continue
                nc.vector.tensor_scalar(
                    out=per_head[k][:, h, :], in0=flat, scalar1=float(h), scalar2=None, op0=ALU.is_equal
                )
            for h in SCALAR_MASKS.get(k, ()):
                if h == 0:
                    nc.scalar.activation(
                        out=per_head[k][:, h, :], in_=flat, func=ACT.Relu, scale=-1.0, bias=plus_one[:, 0:1]
                    )
                elif h == H - 1:
                    nc.scalar.activation(
                        out=per_head[k][:, h, :], in_=flat, func=ACT.Relu, scale=1.0, bias=minus_h[:, H - 2 : H - 1]
                    )
                else:
                    nc.scalar.activation(
                        out=per_head[k][:, h, :], in_=flat, func=ACT.Square, scale=1.0, bias=minus_h[:, h : h + 1]
                    )
                    nc.scalar.activation(
                        out=per_head[k][:, h, :],
                        in_=per_head[k][:, h, :],
                        func=ACT.Relu,
                        scale=-1.0,
                        bias=plus_one[:, 0:1],
                    )

        def masked(k):
            for h in range(H):
                nc.vector.tensor_tensor(
                    out=per_head[k][:, h, :],
                    in0=per_head[k][:, h, :],
                    in1=d_all[k][:].rearrange("p g u t -> p (g u t)"),
                    op=ALU.mult,
                )

        def quantise_d(k):
            d_codes[k] = work.tile([P, H, UNIT_PASSES, P], U32, name="d_codes", tag="d_codes", align_bytes=64)
            d_scales[k] = work.tile([P, H, UNIT_PASSES, P], U8, name="d_scales", tag="d_scales", align_bytes=64)
            for first in range(0, H, HEADS_PER_QUANTISE):
                some = slice(first, first + HEADS_PER_QUANTISE)
                nc.vector.quantize_mx(
                    out=d_codes[k][:, some].rearrange("p h g u -> p (h g u)").bitcast(E5M2_X4),
                    scales=d_scales[k][:, some].rearrange("p h g u -> p (h g u)"),
                    in_=per_head[k][:, some, :].rearrange("p h n -> p (h n)"),
                )

        def multiply(k):
            block = k // BLOCK_UNITS
            if k % BLOCK_UNITS == 0:
                g_sums[block] = [sums.tile([P, E], F32, name="g_sum%d" % h, tag="g_sum%d" % h) for h in range(H)]
            for h in range(H):
                for g in range(UNIT_PASSES):
                    g_all = (k % BLOCK_UNITS) * UNIT_PASSES + g
                    nc.tensor.matmul_mx(
                        out=g_sums[block][h][:],
                        lhsT=d_codes[k][:, h, g, :].bitcast(E5M2_X4),
                        lhsT_scale=d_scales[k][:, h, g, :],
                        rhs=x_codes[:, g_all, :].bitcast(E4M3_X4),
                        rhs_scale=x_scales[:, g_all, :],
                        start=(g_all == 0),
                        stop=(g_all == PASSES - 1),
                    )

        def z_norms(block):
            zn2 = results.tile([P, H], F32, name="zn2", tag="zn2")
            for h in range(H):
                squares = results.tile([P, E], BF16, name="squares", tag="squares", bufs=2)
                nc.scalar.activation(
                    out=squares[:], in_=z_rows[block][:, h, :], func=ACT.Square, accum_out=zn2[:, h : h + 1]
                )
            zn_eps = results.tile([P, H], F32, name="zn_eps", tag="zn_eps")
            nc.gpsimd.tensor_tensor(out=zn_eps[:], in0=zn2[:], in1=exponents[:, 0, :], op=ALU.pow)
            nc.gpsimd.tensor_scalar_add(out=zn_eps[:], in0=zn_eps[:], scalar1=EPS)
            rz = results.tile([P, H], F32, name="rz", tag="rz")
            nc.gpsimd.tensor_tensor(out=rz[:], in0=zn_eps[:], in1=exponents[:, 1, :], op=ALU.pow)
            q_scale[block] = results.tile([P, H], F32, name="q_scale", tag="q_scale")
            nc.gpsimd.tensor_tensor(out=q_scale[block][:], in0=zn2[:], in1=exponents[:, 2, :], op=ALU.pow)
            nc.gpsimd.tensor_tensor(out=q_scale[block][:], in0=q_scale[block][:], in1=rz[:], op=ALU.mult)
            neg_rz[block] = results.tile([P, H], F32, name="neg_rz", tag="neg_rz")
            nc.gpsimd.tensor_scalar_mul(out=neg_rz[block][:], in0=rz[:], scalar1=-1.0)

        def project(block):
            q_dot[block] = results.tile([P, H], F32, name="q_dot", tag="q_dot")
            rest[block] = []
            for first in range(0, H, 2):
                for h in range(first, first + 2):
                    unread = results.tile([P, E], BF16, name="unread", tag="unread", bufs=2)
                    nc.vector.scalar_tensor_tensor(
                        out=unread[:],
                        in0=g_sums[block][h][:],
                        scalar=q_scale[block][:, h : h + 1],
                        in1=z_rows[block][:, h, :],
                        op0=ALU.mult,
                        op1=ALU.mult,
                        accum_out=q_dot[block][:, h : h + 1],
                    )
                for h in range(first, first + 2):
                    rest[block].append(results.tile([P, E], F32, name="rest", tag="rest"))
                    nc.vector.scalar_tensor_tensor(
                        out=rest[block][h][:],
                        in0=z_rows[block][:, h, :],
                        scalar=q_dot[block][:, h : h + 1],
                        in1=g_sums[block][h][:],
                        op0=ALU.mult,
                        op1=ALU.subtract,
                    )

        def finish(block):
            rows = slice(block * P, (block + 1) * P)
            for h in range(H):
                nc.scalar.activation(
                    out=rest[block][h][:], in_=rest[block][h][:], func=ACT.Copy, scale=neg_rz[block][:, h : h + 1]
                )
                nc.scalar.dma_start(out=out[h, rows, :], in_=rest[block][h][:])

        load_x(0)
        load_x(1)
        nc.sync.dma_start(out=rx_rows[0:PLANES, :], in_=rx.rearrange("(j p) -> j p", p=P))
        nc.sync.dma_start(out=beta_b[:], in_=beta.partition_broadcast(P))
        load_m(0)
        load_x(2)
        load_x(3)
        load_m(1)
        load_x(4)
        load_grad(0)
        load_x(5)
        load_x(6)
        load_x(7)
        load_hidx(0)
        load_hidx(1)
        load_grad(1)
        load_z(0)

        group_x(0)
        group_x(1)
        quantise_x(0)
        nc.vector.tensor_copy(out=beta_f[:], in_=beta_b[:])
        nc.vector.tensor_scalar_add(out=beta_m1[:], in0=beta_f[:], scalar1=-1.0)
        rx_bank = turned.tile([P, PACK, P], F32, name="bank", tag="turned")
        nc.tensor.transpose(rx_bank[:, 0, :], rx_rows[:], ident_f[:])
        nc.vector.tensor_scalar(
            out=factor[:],
            in0=rx_bank[:, 0, 0:PLANES],
            scalar1=beta_f[:, 0:1],
            scalar2=0.5,
            op0=ALU.mult,
            op1=ALU.mult,
        )
        logarithms(0)
        logarithms(1)
        nc.scalar.activation(out=ln_factor[:], in_=factor[:], func=ACT.Ln)
        for g in range(2, PASSES):
            group_x(g)
            quantise_x(g - 1)
        quantise_x(PASSES - 1)

        load_m(2)
        load_m(3)
        turn_grad(0)
        exponentials(0)
        winning_heads(0)
        exponentials(1)
        winning_heads(1)
        load_hidx(2)
        load_hidx(3)

        for k in range(UNITS + 1):
            block = k // BLOCK_UNITS
            opens_block = k % BLOCK_UNITS == 0
            more_blocks = block + 1 < USER_BLOCKS
            if opens_block:
                if more_blocks:
                    logarithms(k + 2)
                    logarithms(k + 3)
                if k >= 1:
                    multiply(k - 1)
                if k + 1 < UNITS:
                    turn_grad(k + 1)
            else:
                if k == 1:
                    multiply(k - 1)
                if more_blocks:
                    winning_heads(k + 1)
                    winning_heads(k + 2)
                if k + 1 < UNITS:
                    turn_grad(k + 1)
                if k > 1:
                    multiply(k - 1)
            if k + 2 < UNITS:
                load_grad(k + 2)
            if k < UNITS:
                products(k)
                masks(k)
                masked(k)
                quantise_d(k)
            if opens_block and block >= 1:
                project(block - 1)
            if opens_block:
                if more_blocks:
                    load_z(block + 1)
                    exponentials(k + 2)
                    exponentials(k + 3)
                if block + 2 < USER_BLOCKS:
                    load_m(k + 4)
                    load_m(k + 5)
                if k == UNITS:
                    finish(block - 1)
            else:
                if k == 1:
                    z_norms(0)
                if more_blocks:
                    z_norms(block + 1)
                if block + 2 < USER_BLOCKS:
                    load_hidx(k + 3)
                    load_hidx(k + 4)
                if block >= 1:
                    finish(block - 1)
